import numpy as np
import ml_dtypes

BF16 = ml_dtypes.bfloat16


def bf(x):
    return np.asarray(x, np.float32).astype(BF16)


def f32(x):
    return np.asarray(x, np.float32)


def f64(x):
    return np.asarray(x).astype(np.float64)


def striped(idx):
    return np.tile(idx.reshape(-1, 16).T, (8, 1))


C, S, N = 128, 2048, 256


def setup_inputs():
    return {"x": f32(np.random.standard_normal((C, S))), "lt": bf(np.random.standard_normal((S, N)) / np.sqrt(S)), "tau": f32(0.5 + 0.5 * np.random.uniform(size=(1,))), "offs": striped(np.random.permutation(S)[:N])}


def reference(x, lt, tau, offs):
    idx = offs[:16].T.reshape(-1)
    lap = f64(x) @ f64(lt)
    return f64(x)[:, idx] + (-(f64(tau)[0] * lap))

@@ -1,0 +1,77 @@
+import concourse.mybir as mybir
+from concourse.masks import make_identity
+
+F32 = mybir.dt.float32
+BF16 = mybir.dt.bfloat16
+U16 = mybir.dt.uint16
+MULT = mybir.AluOpType.mult
+ADD = mybir.AluOpType.add
+COPY = mybir.ActivationFunctionType.Copy
+
+P = 128
+S = 2048
+N = 256
+BLOCKS = S // P
+CHUNK = 4
+CHUNKS = BLOCKS // CHUNK
+
+FLOPS = 2 * P * S * N
+
+
+def tile_net_kernel(tc, x, lt, tau, offs, out):
+    nc = tc.nc
+    with (
+        tc.tile_pool(name="held", bufs=1) as held,
+        tc.psum_pool(name="flip", bufs=2) as flip,
+        tc.psum_pool(name="acc", bufs=1) as acc,
+    ):
+        offsets = held.tile([P, N // 16], U16, name="offsets")
+        nc.sync.dma_start(offsets[:], offs)
+
+        x_sb = held.tile([P, S], F32, name="x_sb")
+        for q in range(CHUNKS):
+            cols = slice(q * CHUNK * P, (q + 1) * CHUNK * P)
+            nc.sync.dma_start(x_sb[:, cols], x[:, cols])
+
+        lt_sb = held.tile([P, BLOCKS, N], BF16, name="lt_sb")
+        lt_blocks = lt.rearrange("(b p) n -> p b n", p=P)
+        for q in range(CHUNKS):
+            blocks = slice(q * CHUNK, (q + 1) * CHUNK)
+            nc.sync.dma_start(lt_sb[:, blocks, :], lt_blocks[:, blocks, :])
+
+        tau_sb = held.tile([P, 1], F32, name="tau_sb")
+        nc.scalar.dma_start(tau_sb[:], tau.partition_broadcast(P))
+
+        identity = held.tile([P, P], F32, name="identity")
+        make_identity(nc, identity[:])
+
+        x_flipped = []
+        for q in range(CHUNKS):
+            bank = flip.tile([P, CHUNK * P], F32, name="bank")
+            for i in range(CHUNK):
+                b = q * CHUNK + i
+                nc.tensor.transpose(bank[:, i * P : (i + 1) * P], x_sb[:, b * P : (b + 1) * P], identity[:])
+            flipped = held.tile([P, CHUNK * P], BF16, name=f"flipped{q}")
+            if q % 2 == 0:
+                nc.vector.tensor_copy(flipped[:], bank[:])
+            else:
+                nc.scalar.activation(flipped[:], bank[:], COPY)
+            x_flipped.append(flipped)
+
+        lap = acc.tile([P, N], F32, name="lap")
+        for b in range(BLOCKS):
+            q, i = divmod(b, CHUNK)
+            nc.tensor.matmul(
+                lap[:],
+                x_flipped[q][:, i * P : (i + 1) * P],
+                lt_sb[:, b, :],
+                start=(b == 0),
+                stop=(b == BLOCKS - 1),
+            )
+
+        negated = held.tile([P, N], F32, name="negated")
+        nc.vector.tensor_scalar(negated[:], lap[:], tau_sb[:, 0:1], -1.0, MULT, MULT)
+
+        result = held.tile([P, N], F32, name="result")
+        nc.vector.tensor_tensor(result[:], x_sb[:].indirect(offsets[:]), negated[:], ADD)
+        nc.sync.dma_start(out, result[:])

@@ -34,10 +34,9 @@ def tile_net_kernel(tc, x, lt, tau, offs, out):
             nc.sync.dma_start(x_sb[:, cols], x[:, cols])
 
         lt_sb = held.tile([P, BLOCKS, N], BF16, name="lt_sb")
-        lt_blocks = lt.rearrange("(b p) n -> p b n", p=P)
+        lt_chunks = lt.rearrange("(q p i) n -> p q i n", p=P, i=CHUNK)
         for q in range(CHUNKS):
-            blocks = slice(q * CHUNK, (q + 1) * CHUNK)
-            nc.sync.dma_start(lt_sb[:, blocks, :], lt_blocks[:, blocks, :])
+            nc.sync.dma_start(lt_sb[:, q * CHUNK : (q + 1) * CHUNK, :], lt_chunks[:, q, :, :])
 
         tau_sb = held.tile([P, 1], F32, name="tau_sb")
         nc.scalar.dma_start(tau_sb[:], tau.partition_broadcast(P))
@@ -45,12 +44,12 @@ def tile_net_kernel(tc, x, lt, tau, offs, out):
         identity = held.tile([P, P], F32, name="identity")
         make_identity(nc, identity[:])
 
+        x_blocks = x_sb[:].rearrange("c (q p i) -> c q i p", p=P, i=CHUNK)
         x_flipped = []
         for q in range(CHUNKS):
             bank = flip.tile([P, CHUNK * P], F32, name="bank")
             for i in range(CHUNK):
-                b = q * CHUNK + i
-                nc.tensor.transpose(bank[:, i * P : (i + 1) * P], x_sb[:, b * P : (b + 1) * P], identity[:])
+                nc.tensor.transpose(bank[:, i * P : (i + 1) * P], x_blocks[:, q, i, :], identity[:])
             flipped = held.tile([P, CHUNK * P], BF16, name=f"flipped{q}")
             if q % 2 == 0:
                 nc.vector.tensor_copy(flipped[:], bank[:])

@@ -34,27 +34,26 @@ def tile_net_kernel(tc, x, lt, tau, offs, out):
             nc.sync.dma_start(x_sb[:, cols], x[:, cols])
 
         lt_sb = held.tile([P, BLOCKS, N], BF16, name="lt_sb")
-        lt_chunks = lt.rearrange("(q p i) n -> p q i n", p=P, i=CHUNK)
+        lt_blocks = lt.rearrange("(b p) n -> p b n", p=P)
         for q in range(CHUNKS):
-            nc.sync.dma_start(lt_sb[:, q * CHUNK : (q + 1) * CHUNK, :], lt_chunks[:, q, :, :])
+            blocks = slice(q * CHUNK, (q + 1) * CHUNK)
+            nc.sync.dma_start(lt_sb[:, blocks, :], lt_blocks[:, blocks, :])
 
         tau_sb = held.tile([P, 1], F32, name="tau_sb")
         nc.scalar.dma_start(tau_sb[:], tau.partition_broadcast(P))
 
-        identity = held.tile([P, P], F32, name="identity")
+        identity = held.tile([P, P], BF16, name="identity")
         make_identity(nc, identity[:])
 
-        x_blocks = x_sb[:].rearrange("c (q p i) -> c q i p", p=P, i=CHUNK)
         x_flipped = []
         for q in range(CHUNKS):
-            bank = flip.tile([P, CHUNK * P], F32, name="bank")
+            rounded = held.tile([P, CHUNK * P], BF16, name=f"rounded{q}")
+            nc.vector.tensor_copy(rounded[:], x_sb[:, q * CHUNK * P : (q + 1) * CHUNK * P])
+            bank = flip.tile([P, CHUNK * P], BF16, name="bank")
             for i in range(CHUNK):
-                nc.tensor.transpose(bank[:, i * P : (i + 1) * P], x_blocks[:, q, i, :], identity[:])
+                nc.tensor.transpose(bank[:, i * P : (i + 1) * P], rounded[:, i * P : (i + 1) * P], identity[:])
             flipped = held.tile([P, CHUNK * P], BF16, name=f"flipped{q}")
-            if q % 2 == 0:
-                nc.vector.tensor_copy(flipped[:], bank[:])
-            else:
-                nc.scalar.activation(flipped[:], bank[:], COPY)
+            nc.scalar.activation(flipped[:], bank[:], COPY)
             x_flipped.append(flipped)
 
         lap = acc.tile([P, N], F32, name="lap")

@@ -15,6 +15,9 @@ BLOCKS = S // P
 CHUNK = 4
 CHUNKS = BLOCKS // CHUNK
 
+WARM_COLS = 512
+WARM_MATMULS = 4
+
 FLOPS = 2 * P * S * N
 
 
@@ -24,29 +27,42 @@ def tile_net_kernel(tc, x, lt, tau, offs, out):
         tc.tile_pool(name="held", bufs=1) as held,
         tc.psum_pool(name="flip", bufs=2) as flip,
         tc.psum_pool(name="acc", bufs=1) as acc,
+        tc.psum_pool(name="warm", bufs=1) as warm,
     ):
         offsets = held.tile([P, N // 16], U16, name="offsets")
         nc.sync.dma_start(offsets[:], offs)
 
         x_sb = held.tile([P, S], F32, name="x_sb")
-        for q in range(CHUNKS):
+        lt_sb = held.tile([P, BLOCKS, N], BF16, name="lt_sb")
+        lt_blocks = lt.rearrange("(b p) n -> p b n", p=P)
+
+        def load_x(q):
             cols = slice(q * CHUNK * P, (q + 1) * CHUNK * P)
             nc.sync.dma_start(x_sb[:, cols], x[:, cols])
 
-        lt_sb = held.tile([P, BLOCKS, N], BF16, name="lt_sb")
-        lt_blocks = lt.rearrange("(b p) n -> p b n", p=P)
-        for q in range(CHUNKS):
+        def load_lt(q):
             blocks = slice(q * CHUNK, (q + 1) * CHUNK)
             nc.sync.dma_start(lt_sb[:, blocks, :], lt_blocks[:, blocks, :])
+
+        load_x(0)
+        for q in range(CHUNKS):
+            if q + 1 < CHUNKS:
+                load_x(q + 1)
+            load_lt(q)
 
         tau_sb = held.tile([P, 1], F32, name="tau_sb")
         nc.scalar.dma_start(tau_sb[:], tau.partition_broadcast(P))
 
+        zeros = held.tile([P, WARM_COLS], BF16, name="zeros")
+        nc.vector.memset(zeros[:], 0.0)
+        unused = warm.tile([P, WARM_COLS], F32, name="unused")
+        for w in range(WARM_MATMULS):
+            nc.tensor.matmul(unused[:], zeros[:, 0:P], zeros[:], start=True, stop=True)
+
         identity = held.tile([P, P], BF16, name="identity")
         make_identity(nc, identity[:])
 
-        x_flipped = []
-        for q in range(CHUNKS):
+        def flip_x(q):
             rounded = held.tile([P, CHUNK * P], BF16, name=f"rounded{q}")
             nc.vector.tensor_copy(rounded[:], x_sb[:, q * CHUNK * P : (q + 1) * CHUNK * P])
             bank = flip.tile([P, CHUNK * P], BF16, name="bank")
@@ -54,18 +70,26 @@ def tile_net_kernel(tc, x, lt, tau, offs, out):
                 nc.tensor.transpose(bank[:, i * P : (i + 1) * P], rounded[:, i * P : (i + 1) * P], identity[:])
             flipped = held.tile([P, CHUNK * P], BF16, name=f"flipped{q}")
             nc.scalar.activation(flipped[:], bank[:], COPY)
-            x_flipped.append(flipped)
+            return flipped
 
         lap = acc.tile([P, N], F32, name="lap")
-        for b in range(BLOCKS):
-            q, i = divmod(b, CHUNK)
-            nc.tensor.matmul(
-                lap[:],
-                x_flipped[q][:, i * P : (i + 1) * P],
-                lt_sb[:, b, :],
-                start=(b == 0),
-                stop=(b == BLOCKS - 1),
-            )
+
+        def multiply(q, flipped):
+            for i in range(CHUNK):
+                b = q * CHUNK + i
+                nc.tensor.matmul(
+                    lap[:],
+                    flipped[:, i * P : (i + 1) * P],
+                    lt_sb[:, b, :],
+                    start=(b == 0),
+                    stop=(b == BLOCKS - 1),
+                )
+
+        x_flipped = [flip_x(0)]
+        for q in range(CHUNKS):
+            if q + 1 < CHUNKS:
+                x_flipped.append(flip_x(q + 1))
+            multiply(q, x_flipped[q])
 
         negated = held.tile([P, N], F32, name="negated")
         nc.vector.tensor_scalar(negated[:], lap[:], tau_sb[:, 0:1], -1.0, MULT, MULT)

@@ -15,9 +15,6 @@ BLOCKS = S // P
 CHUNK = 4
 CHUNKS = BLOCKS // CHUNK
 
-WARM_COLS = 512
-WARM_MATMULS = 4
-
 FLOPS = 2 * P * S * N
 
 
@@ -27,69 +24,48 @@ def tile_net_kernel(tc, x, lt, tau, offs, out):
         tc.tile_pool(name="held", bufs=1) as held,
         tc.psum_pool(name="flip", bufs=2) as flip,
         tc.psum_pool(name="acc", bufs=1) as acc,
-        tc.psum_pool(name="warm", bufs=1) as warm,
     ):
         offsets = held.tile([P, N // 16], U16, name="offsets")
         nc.sync.dma_start(offsets[:], offs)
 
         x_sb = held.tile([P, S], F32, name="x_sb")
-        lt_sb = held.tile([P, BLOCKS, N], BF16, name="lt_sb")
-        lt_blocks = lt.rearrange("(b p) n -> p b n", p=P)
-
-        def load_x(q):
+        for q in range(CHUNKS):
             cols = slice(q * CHUNK * P, (q + 1) * CHUNK * P)
             nc.sync.dma_start(x_sb[:, cols], x[:, cols])
 
-        def load_lt(q):
-            blocks = slice(q * CHUNK, (q + 1) * CHUNK)
-            nc.sync.dma_start(lt_sb[:, blocks, :], lt_blocks[:, blocks, :])
-
-        load_x(0)
+        lt_sb = held.tile([P, BLOCKS, N], BF16, name="lt_sb")
+        lt_chunks = lt.rearrange("(q p i) n -> p q i n", p=P, i=CHUNK)
         for q in range(CHUNKS):
-            if q + 1 < CHUNKS:
-                load_x(q + 1)
-            load_lt(q)
+            nc.sync.dma_start(lt_sb[:, q * CHUNK : (q + 1) * CHUNK, :], lt_chunks[:, q, :, :])
 
         tau_sb = held.tile([P, 1], F32, name="tau_sb")
         nc.scalar.dma_start(tau_sb[:], tau.partition_broadcast(P))
 
-        zeros = held.tile([P, WARM_COLS], BF16, name="zeros")
-        nc.vector.memset(zeros[:], 0.0)
-        unused = warm.tile([P, WARM_COLS], F32, name="unused")
-        for w in range(WARM_MATMULS):
-            nc.tensor.matmul(unused[:], zeros[:, 0:P], zeros[:], start=True, stop=True)
-
         identity = held.tile([P, P], BF16, name="identity")
         make_identity(nc, identity[:])
 
-        def flip_x(q):
+        x_flipped = []
+        for q in range(CHUNKS):
             rounded = held.tile([P, CHUNK * P], BF16, name=f"rounded{q}")
             nc.vector.tensor_copy(rounded[:], x_sb[:, q * CHUNK * P : (q + 1) * CHUNK * P])
+            blocks = rounded[:].rearrange("c (p i) -> c i p", i=CHUNK)
             bank = flip.tile([P, CHUNK * P], BF16, name="bank")
             for i in range(CHUNK):
-                nc.tensor.transpose(bank[:, i * P : (i + 1) * P], rounded[:, i * P : (i + 1) * P], identity[:])
+                nc.tensor.transpose(bank[:, i * P : (i + 1) * P], blocks[:, i, :], identity[:])
             flipped = held.tile([P, CHUNK * P], BF16, name=f"flipped{q}")
             nc.scalar.activation(flipped[:], bank[:], COPY)
-            return flipped
+            x_flipped.append(flipped)
 
         lap = acc.tile([P, N], F32, name="lap")
-
-        def multiply(q, flipped):
-            for i in range(CHUNK):
-                b = q * CHUNK + i
-                nc.tensor.matmul(
-                    lap[:],
-                    flipped[:, i * P : (i + 1) * P],
-                    lt_sb[:, b, :],
-                    start=(b == 0),
-                    stop=(b == BLOCKS - 1),
-                )
-
-        x_flipped = [flip_x(0)]
-        for q in range(CHUNKS):
-            if q + 1 < CHUNKS:
-                x_flipped.append(flip_x(q + 1))
-            multiply(q, x_flipped[q])
+        for b in range(BLOCKS):
+            q, i = divmod(b, CHUNK)
+            nc.tensor.matmul(
+                lap[:],
+                x_flipped[q][:, i * P : (i + 1) * P],
+                lt_sb[:, b, :],
+                start=(b == 0),
+                stop=(b == BLOCKS - 1),
+            )
 
         negated = held.tile([P, N], F32, name="negated")
         nc.vector.tensor_scalar(negated[:], lap[:], tau_sb[:, 0:1], -1.0, MULT, MULT)

@@ -14,6 +14,8 @@ N = 256
 BLOCKS = S // P
 CHUNK = 4
 CHUNKS = BLOCKS // CHUNK
+HALVES = 2
+HALF = N // HALVES
 
 FLOPS = 2 * P * S * N
 
@@ -40,6 +42,8 @@ def tile_net_kernel(tc, x, lt, tau, offs, out):
 
         tau_sb = held.tile([P, 1], F32, name="tau_sb")
         nc.scalar.dma_start(tau_sb[:], tau.partition_broadcast(P))
+        neg_tau = held.tile([P, 1], F32, name="neg_tau")
+        nc.vector.tensor_scalar_mul(neg_tau[:], tau_sb[:], -1.0)
 
         identity = held.tile([P, P], BF16, name="identity")
         make_identity(nc, identity[:])
@@ -56,20 +60,24 @@ def tile_net_kernel(tc, x, lt, tau, offs, out):
             nc.scalar.activation(flipped[:], bank[:], COPY)
             x_flipped.append(flipped)
 
-        lap = acc.tile([P, N], F32, name="lap")
-        for b in range(BLOCKS):
-            q, i = divmod(b, CHUNK)
-            nc.tensor.matmul(
-                lap[:],
-                x_flipped[q][:, i * P : (i + 1) * P],
-                lt_sb[:, b, :],
-                start=(b == 0),
-                stop=(b == BLOCKS - 1),
-            )
+        lap = [acc.tile([P, HALF], F32, name=f"lap{h}") for h in range(HALVES)]
+        for q in range(CHUNKS):
+            for h in range(HALVES):
+                for i in range(CHUNK):
+                    b = q * CHUNK + i
+                    nc.tensor.matmul(
+                        lap[h][:],
+                        x_flipped[q][:, i * P : (i + 1) * P],
+                        lt_sb[:, b, h * HALF : (h + 1) * HALF],
+                        start=(b == 0),
+                        stop=(b == BLOCKS - 1),
+                    )
 
-        negated = held.tile([P, N], F32, name="negated")
-        nc.vector.tensor_scalar(negated[:], lap[:], tau_sb[:, 0:1], -1.0, MULT, MULT)
+        for h in range(HALVES):
+            negated = held.tile([P, HALF], F32, name=f"negated{h}")
+            nc.scalar.activation(negated[:], lap[h][:], COPY, scale=neg_tau[:, 0:1])
 
-        result = held.tile([P, N], F32, name="result")
-        nc.vector.tensor_tensor(result[:], x_sb[:].indirect(offsets[:]), negated[:], ADD)
-        nc.sync.dma_start(out, result[:])
+            piece = offsets[:, h * HALF // 16 : (h + 1) * HALF // 16]
+            result = held.tile([P, HALF], F32, name=f"result{h}")
+            nc.vector.tensor_tensor(result[:], x_sb[:].indirect(piece), negated[:], ADD)
+            nc.sync.dma_start(out[:, h * HALF : (h + 1) * HALF], result[:])

@@ -14,8 +14,8 @@ N = 256
 BLOCKS = S // P
 CHUNK = 4
 CHUNKS = BLOCKS // CHUNK
-HALVES = 2
-HALF = N // HALVES
+
+WARM_MATMULS = 4
 
 FLOPS = 2 * P * S * N
 
@@ -26,6 +26,7 @@ def tile_net_kernel(tc, x, lt, tau, offs, out):
         tc.tile_pool(name="held", bufs=1) as held,
         tc.psum_pool(name="flip", bufs=2) as flip,
         tc.psum_pool(name="acc", bufs=1) as acc,
+        tc.psum_pool(name="warm", bufs=1) as warm,
     ):
         offsets = held.tile([P, N // 16], U16, name="offsets")
         nc.sync.dma_start(offsets[:], offs)
@@ -42,8 +43,16 @@ def tile_net_kernel(tc, x, lt, tau, offs, out):
 
         tau_sb = held.tile([P, 1], F32, name="tau_sb")
         nc.scalar.dma_start(tau_sb[:], tau.partition_broadcast(P))
-        neg_tau = held.tile([P, 1], F32, name="neg_tau")
-        nc.vector.tensor_scalar_mul(neg_tau[:], tau_sb[:], -1.0)
+
+        zeros = held.tile([P, CHUNK * P], BF16, name="zeros")
+        nc.vector.memset(zeros[:], 0.0)
+        unused = warm.tile([P, CHUNK * P], F32, name="unused")
+
+        def keep_busy(moving):
+            nc.tensor.matmul(unused[:], zeros[:, 0:P], moving, start=True, stop=True)
+
+        for w in range(WARM_MATMULS):
+            keep_busy(zeros[:])
 
         identity = held.tile([P, P], BF16, name="identity")
         make_identity(nc, identity[:])
@@ -56,28 +65,25 @@ def tile_net_kernel(tc, x, lt, tau, offs, out):
             bank = flip.tile([P, CHUNK * P], BF16, name="bank")
             for i in range(CHUNK):
                 nc.tensor.transpose(bank[:, i * P : (i + 1) * P], blocks[:, i, :], identity[:])
+            keep_busy(rounded[:])
             flipped = held.tile([P, CHUNK * P], BF16, name=f"flipped{q}")
             nc.scalar.activation(flipped[:], bank[:], COPY)
             x_flipped.append(flipped)
 
-        lap = [acc.tile([P, HALF], F32, name=f"lap{h}") for h in range(HALVES)]
-        for q in range(CHUNKS):
-            for h in range(HALVES):
-                for i in range(CHUNK):
-                    b = q * CHUNK + i
-                    nc.tensor.matmul(
-                        lap[h][:],
-                        x_flipped[q][:, i * P : (i + 1) * P],
-                        lt_sb[:, b, h * HALF : (h + 1) * HALF],
-                        start=(b == 0),
-                        stop=(b == BLOCKS - 1),
-                    )
+        lap = acc.tile([P, N], F32, name="lap")
+        for b in range(BLOCKS):
+            q, i = divmod(b, CHUNK)
+            nc.tensor.matmul(
+                lap[:],
+                x_flipped[q][:, i * P : (i + 1) * P],
+                lt_sb[:, b, :],
+                start=(b == 0),
+                stop=(b == BLOCKS - 1),
+            )
 
-        for h in range(HALVES):
-            negated = held.tile([P, HALF], F32, name=f"negated{h}")
-            nc.scalar.activation(negated[:], lap[h][:], COPY, scale=neg_tau[:, 0:1])
+        negated = held.tile([P, N], F32, name="negated")
+        nc.vector.tensor_scalar(negated[:], lap[:], tau_sb[:, 0:1], -1.0, MULT, MULT)
 
-            piece = offsets[:, h * HALF // 16 : (h + 1) * HALF // 16]
-            result = held.tile([P, HALF], F32, name=f"result{h}")
-            nc.vector.tensor_tensor(result[:], x_sb[:].indirect(piece), negated[:], ADD)
-            nc.sync.dma_start(out[:, h * HALF : (h + 1) * HALF], result[:])
+        result = held.tile([P, N], F32, name="result")
+        nc.vector.tensor_tensor(result[:], x_sb[:].indirect(offsets[:]), negated[:], ADD)
+        nc.sync.dma_start(out, result[:])

@@ -14,8 +14,8 @@ N = 256
 BLOCKS = S // P
 CHUNK = 4
 CHUNKS = BLOCKS // CHUNK
-
-WARM_MATMULS = 4
+PAIR = 2
+WORDS = CHUNK // PAIR
 
 FLOPS = 2 * P * S * N
 
@@ -24,58 +24,46 @@ def tile_net_kernel(tc, x, lt, tau, offs, out):
     nc = tc.nc
     with (
         tc.tile_pool(name="held", bufs=1) as held,
-        tc.psum_pool(name="flip", bufs=2) as flip,
+        tc.psum_pool(name="flip", bufs=4) as flip,
         tc.psum_pool(name="acc", bufs=1) as acc,
-        tc.psum_pool(name="warm", bufs=1) as warm,
     ):
-        offsets = held.tile([P, N // 16], U16, name="offsets")
-        nc.sync.dma_start(offsets[:], offs)
-
         x_sb = held.tile([P, S], F32, name="x_sb")
         for q in range(CHUNKS):
             cols = slice(q * CHUNK * P, (q + 1) * CHUNK * P)
             nc.sync.dma_start(x_sb[:, cols], x[:, cols])
+
+        offsets = held.tile([P, N // 16], U16, name="offsets")
+        nc.sync.dma_start(offsets[:], offs)
+        tau_sb = held.tile([P, 1], F32, name="tau_sb")
+        nc.sync.dma_start(tau_sb[:], tau.partition_broadcast(P))
 
         lt_sb = held.tile([P, BLOCKS, N], BF16, name="lt_sb")
         lt_chunks = lt.rearrange("(q p i) n -> p q i n", p=P, i=CHUNK)
         for q in range(CHUNKS):
             nc.sync.dma_start(lt_sb[:, q * CHUNK : (q + 1) * CHUNK, :], lt_chunks[:, q, :, :])
 
-        tau_sb = held.tile([P, 1], F32, name="tau_sb")
-        nc.scalar.dma_start(tau_sb[:], tau.partition_broadcast(P))
-
-        zeros = held.tile([P, CHUNK * P], BF16, name="zeros")
-        nc.vector.memset(zeros[:], 0.0)
-        unused = warm.tile([P, CHUNK * P], F32, name="unused")
-
-        def keep_busy(moving):
-            nc.tensor.matmul(unused[:], zeros[:, 0:P], moving, start=True, stop=True)
-
-        for w in range(WARM_MATMULS):
-            keep_busy(zeros[:])
-
-        identity = held.tile([P, P], BF16, name="identity")
+        identity = held.tile([P, P], F32, name="identity")
         make_identity(nc, identity[:])
 
         x_flipped = []
         for q in range(CHUNKS):
             rounded = held.tile([P, CHUNK * P], BF16, name=f"rounded{q}")
             nc.vector.tensor_copy(rounded[:], x_sb[:, q * CHUNK * P : (q + 1) * CHUNK * P])
-            blocks = rounded[:].rearrange("c (p i) -> c i p", i=CHUNK)
-            bank = flip.tile([P, CHUNK * P], BF16, name="bank")
-            for i in range(CHUNK):
-                nc.tensor.transpose(bank[:, i * P : (i + 1) * P], blocks[:, i, :], identity[:])
-            keep_busy(rounded[:])
+            words = rounded[:].bitcast(F32).rearrange("c (k t) -> c t k", t=WORDS)
+            bank = flip.tile([P, WORDS * P], F32, name="bank")
+            for t in range(WORDS):
+                nc.tensor.transpose(bank[:, t * P : (t + 1) * P], words[:, t, :], identity[:])
             flipped = held.tile([P, CHUNK * P], BF16, name=f"flipped{q}")
-            nc.scalar.activation(flipped[:], bank[:], COPY)
-            x_flipped.append(flipped)
+            nc.scalar.activation(flipped[:], bank[:].bitcast(BF16), COPY)
+            x_flipped.append(flipped[:].rearrange("k (t c e) -> k t e c", c=P, e=PAIR))
 
         lap = acc.tile([P, N], F32, name="lap")
         for b in range(BLOCKS):
             q, i = divmod(b, CHUNK)
+            t, e = divmod(i, PAIR)
             nc.tensor.matmul(
                 lap[:],
-                x_flipped[q][:, i * P : (i + 1) * P],
+                x_flipped[q][:, t, e, :],
                 lt_sb[:, b, :],
                 start=(b == 0),
                 stop=(b == BLOCKS - 1),

@@ -14,8 +14,6 @@ N = 256
 BLOCKS = S // P
 CHUNK = 4
 CHUNKS = BLOCKS // CHUNK
-PAIR = 2
-WORDS = CHUNK // PAIR
 
 FLOPS = 2 * P * S * N
 
@@ -42,28 +40,27 @@ def tile_net_kernel(tc, x, lt, tau, offs, out):
         for q in range(CHUNKS):
             nc.sync.dma_start(lt_sb[:, q * CHUNK : (q + 1) * CHUNK, :], lt_chunks[:, q, :, :])
 
-        identity = held.tile([P, P], F32, name="identity")
+        identity = held.tile([P, P], BF16, name="identity")
         make_identity(nc, identity[:])
 
         x_flipped = []
         for q in range(CHUNKS):
             rounded = held.tile([P, CHUNK * P], BF16, name=f"rounded{q}")
             nc.vector.tensor_copy(rounded[:], x_sb[:, q * CHUNK * P : (q + 1) * CHUNK * P])
-            words = rounded[:].bitcast(F32).rearrange("c (k t) -> c t k", t=WORDS)
-            bank = flip.tile([P, WORDS * P], F32, name="bank")
-            for t in range(WORDS):
-                nc.tensor.transpose(bank[:, t * P : (t + 1) * P], words[:, t, :], identity[:])
+            blocks = rounded[:].rearrange("c (k i) -> c i k", i=CHUNK)
+            bank = flip.tile([P, CHUNK * P], F32, name="bank")
+            for i in range(CHUNK):
+                nc.tensor.matmul(bank[:, i * P : (i + 1) * P], blocks[:, i, :], identity[:], start=True, stop=True)
             flipped = held.tile([P, CHUNK * P], BF16, name=f"flipped{q}")
-            nc.scalar.activation(flipped[:], bank[:].bitcast(BF16), COPY)
-            x_flipped.append(flipped[:].rearrange("k (t c e) -> k t e c", c=P, e=PAIR))
+            nc.scalar.activation(flipped[:], bank[:], COPY)
+            x_flipped.append(flipped)
 
         lap = acc.tile([P, N], F32, name="lap")
         for b in range(BLOCKS):
             q, i = divmod(b, CHUNK)
-            t, e = divmod(i, PAIR)
             nc.tensor.matmul(
                 lap[:],
-                x_flipped[q][:, t, e, :],
+                x_flipped[q][:, i * P : (i + 1) * P],
                 lt_sb[:, b, :],
                 start=(b == 0),
                 stop=(b == BLOCKS - 1),

@@ -11,9 +11,9 @@ COPY = mybir.ActivationFunctionType.Copy
 P = 128
 S = 2048
 N = 256
-BLOCKS = S // P
-CHUNK = 4
-CHUNKS = BLOCKS // CHUNK
+X_LOADS = 4
+GROUPS = (4, 4, 4, 2, 2)
+assert sum(GROUPS) * P == S
 
 FLOPS = 2 * P * S * N
 
@@ -26,8 +26,8 @@ def tile_net_kernel(tc, x, lt, tau, offs, out):
         tc.psum_pool(name="acc", bufs=1) as acc,
     ):
         x_sb = held.tile([P, S], F32, name="x_sb")
-        for q in range(CHUNKS):
-            cols = slice(q * CHUNK * P, (q + 1) * CHUNK * P)
+        for q in range(X_LOADS):
+            cols = slice(q * S // X_LOADS, (q + 1) * S // X_LOADS)
             nc.sync.dma_start(x_sb[:, cols], x[:, cols])
 
         offsets = held.tile([P, N // 16], U16, name="offsets")
@@ -35,36 +35,39 @@ def tile_net_kernel(tc, x, lt, tau, offs, out):
         tau_sb = held.tile([P, 1], F32, name="tau_sb")
         nc.sync.dma_start(tau_sb[:], tau.partition_broadcast(P))
 
-        lt_sb = held.tile([P, BLOCKS, N], BF16, name="lt_sb")
-        lt_chunks = lt.rearrange("(q p i) n -> p q i n", p=P, i=CHUNK)
-        for q in range(CHUNKS):
-            nc.sync.dma_start(lt_sb[:, q * CHUNK : (q + 1) * CHUNK, :], lt_chunks[:, q, :, :])
+        firsts = [sum(GROUPS[:g]) * P for g in range(len(GROUPS))]
+        lt_groups = []
+        for g, (first, m) in enumerate(zip(firsts, GROUPS)):
+            lt_group = held.tile([P, m, N], BF16, name=f"lt_group{g}")
+            rows = lt[first : first + m * P, :].rearrange("(p i) n -> p i n", i=m)
+            nc.sync.dma_start(lt_group[:], rows)
+            lt_groups.append(lt_group)
 
         identity = held.tile([P, P], BF16, name="identity")
         make_identity(nc, identity[:])
 
         x_flipped = []
-        for q in range(CHUNKS):
-            rounded = held.tile([P, CHUNK * P], BF16, name=f"rounded{q}")
-            nc.vector.tensor_copy(rounded[:], x_sb[:, q * CHUNK * P : (q + 1) * CHUNK * P])
-            blocks = rounded[:].rearrange("c (k i) -> c i k", i=CHUNK)
-            bank = flip.tile([P, CHUNK * P], F32, name="bank")
-            for i in range(CHUNK):
+        for g, (first, m) in enumerate(zip(firsts, GROUPS)):
+            rounded = held.tile([P, m * P], BF16, name=f"rounded{g}")
+            nc.vector.tensor_copy(rounded[:], x_sb[:, first : first + m * P])
+            blocks = rounded[:].rearrange("c (k i) -> c i k", i=m)
+            bank = flip.tile([P, max(GROUPS) * P], F32, name="bank")
+            for i in range(m):
                 nc.tensor.matmul(bank[:, i * P : (i + 1) * P], blocks[:, i, :], identity[:], start=True, stop=True)
-            flipped = held.tile([P, CHUNK * P], BF16, name=f"flipped{q}")
-            nc.scalar.activation(flipped[:], bank[:], COPY)
+            flipped = held.tile([P, m * P], BF16, name=f"flipped{g}")
+            nc.scalar.activation(flipped[:], bank[:, : m * P], COPY)
             x_flipped.append(flipped)
 
         lap = acc.tile([P, N], F32, name="lap")
-        for b in range(BLOCKS):
-            q, i = divmod(b, CHUNK)
-            nc.tensor.matmul(
-                lap[:],
-                x_flipped[q][:, i * P : (i + 1) * P],
-                lt_sb[:, b, :],
-                start=(b == 0),
-                stop=(b == BLOCKS - 1),
-            )
+        for g, m in enumerate(GROUPS):
+            for i in range(m):
+                nc.tensor.matmul(
+                    lap[:],
+                    x_flipped[g][:, i * P : (i + 1) * P],
+                    lt_groups[g][:, i, :],
+                    start=(g == 0 and i == 0),
+                    stop=(g == len(GROUPS) - 1 and i == m - 1),
+                )
 
         negated = held.tile([P, N], F32, name="negated")
         nc.vector.tensor_scalar(negated[:], lap[:], tau_sb[:, 0:1], -1.0, MULT, MULT)

@@ -11,6 +11,9 @@ COPY = mybir.ActivationFunctionType.Copy
 P = 128
 S = 2048
 N = 256
+HALVES = 2
+H = N // HALVES
+BANK = 512
 X_LOADS = 4
 GROUPS = (4, 4, 4, 2, 2)
 assert sum(GROUPS) * P == S
@@ -58,20 +61,25 @@ def tile_net_kernel(tc, x, lt, tau, offs, out):
             nc.scalar.activation(flipped[:], bank[:, : m * P], COPY)
             x_flipped.append(flipped)
 
-        lap = acc.tile([P, N], F32, name="lap")
+        laps = [acc.tile([P, BANK], F32, name=f"lap{h}") for h in range(HALVES)]
         for g, m in enumerate(GROUPS):
-            for i in range(m):
-                nc.tensor.matmul(
-                    lap[:],
-                    x_flipped[g][:, i * P : (i + 1) * P],
-                    lt_groups[g][:, i, :],
-                    start=(g == 0 and i == 0),
-                    stop=(g == len(GROUPS) - 1 and i == m - 1),
-                )
+            for h in range(HALVES):
+                for i in range(m):
+                    nc.tensor.matmul(
+                        laps[h][:, :H],
+                        x_flipped[g][:, i * P : (i + 1) * P],
+                        lt_groups[g][:, i, h * H : (h + 1) * H],
+                        start=(g == 0 and i == 0),
+                        stop=(g == len(GROUPS) - 1 and i == m - 1),
+                    )
 
         negated = held.tile([P, N], F32, name="negated")
-        nc.vector.tensor_scalar(negated[:], lap[:], tau_sb[:, 0:1], -1.0, MULT, MULT)
+        for h in range(HALVES):
+            nc.vector.tensor_scalar(negated[:, h * H : (h + 1) * H], laps[h][:, :H], tau_sb[:, 0:1], -1.0, MULT, MULT)
 
         result = held.tile([P, N], F32, name="result")
-        nc.vector.tensor_tensor(result[:], x_sb[:].indirect(offsets[:]), negated[:], ADD)
-        nc.sync.dma_start(out, result[:])
+        for h in range(HALVES):
+            cols = slice(h * H, (h + 1) * H)
+            picked = x_sb[:].indirect(offsets[:, h * H // 16 : (h + 1) * H // 16])
+            nc.vector.tensor_tensor(result[:, cols], picked, negated[:, cols], ADD)
+            nc.sync.dma_start(out[:, cols], result[:, cols])

@@ -14,7 +14,8 @@ N = 256
 HALVES = 2
 H = N // HALVES
 BANK = 512
-X_LOADS = 4
+X_LOADS = (512, 512, 1024)
+assert sum(X_LOADS) == S
 GROUPS = (4, 4, 4, 2, 2)
 assert sum(GROUPS) * P == S
 
@@ -29,8 +30,8 @@ def tile_net_kernel(tc, x, lt, tau, offs, out):
         tc.psum_pool(name="acc", bufs=1) as acc,
     ):
         x_sb = held.tile([P, S], F32, name="x_sb")
-        for q in range(X_LOADS):
-            cols = slice(q * S // X_LOADS, (q + 1) * S // X_LOADS)
+        for q, width in enumerate(X_LOADS):
+            cols = slice(sum(X_LOADS[:q]), sum(X_LOADS[:q]) + width)
             nc.sync.dma_start(x_sb[:, cols], x[:, cols])
 
         offsets = held.tile([P, N // 16], U16, name="offsets")

@@ -34,11 +34,6 @@ def tile_net_kernel(tc, x, lt, tau, offs, out):
             cols = slice(sum(X_LOADS[:q]), sum(X_LOADS[:q]) + width)
             nc.sync.dma_start(x_sb[:, cols], x[:, cols])
 
-        offsets = held.tile([P, N // 16], U16, name="offsets")
-        nc.sync.dma_start(offsets[:], offs)
-        tau_sb = held.tile([P, 1], F32, name="tau_sb")
-        nc.sync.dma_start(tau_sb[:], tau.partition_broadcast(P))
-
         firsts = [sum(GROUPS[:g]) * P for g in range(len(GROUPS))]
         lt_groups = []
         for g, (first, m) in enumerate(zip(firsts, GROUPS)):
@@ -46,6 +41,11 @@ def tile_net_kernel(tc, x, lt, tau, offs, out):
             rows = lt[first : first + m * P, :].rearrange("(p i) n -> p i n", i=m)
             nc.sync.dma_start(lt_group[:], rows)
             lt_groups.append(lt_group)
+
+        tau_sb = held.tile([P, 1], F32, name="tau_sb")
+        nc.sync.dma_start(tau_sb[:], tau.partition_broadcast(P))
+        offsets = held.tile([P, N // 16], U16, name="offsets")
+        nc.sync.dma_start(offsets[:], offs)
 
         identity = held.tile([P, P], BF16, name="identity")
         make_identity(nc, identity[:])

@@ -14,7 +14,7 @@ N = 256
 HALVES = 2
 H = N // HALVES
 BANK = 512
-X_LOADS = (512, 512, 1024)
+X_LOADS = (512, 512, 512, 512)
 assert sum(X_LOADS) == S
 GROUPS = (4, 4, 4, 2, 2)
 assert sum(GROUPS) * P == S

@@ -6,7 +6,6 @@ BF16 = mybir.dt.bfloat16
 U16 = mybir.dt.uint16
 MULT = mybir.AluOpType.mult
 ADD = mybir.AluOpType.add
-COPY = mybir.ActivationFunctionType.Copy
 
 P = 128
 S = 2048
@@ -55,24 +54,26 @@ def tile_net_kernel(tc, x, lt, tau, offs, out):
             rounded = held.tile([P, m * P], BF16, name=f"rounded{g}")
             nc.vector.tensor_copy(rounded[:], x_sb[:, first : first + m * P])
             blocks = rounded[:].rearrange("c (k i) -> c i k", i=m)
-            bank = flip.tile([P, max(GROUPS) * P], F32, name="bank")
+            bank = flip.tile([P, 2 * BANK], BF16, name="bank")
             for i in range(m):
                 nc.tensor.matmul(bank[:, i * P : (i + 1) * P], blocks[:, i, :], identity[:], start=True, stop=True)
             flipped = held.tile([P, m * P], BF16, name=f"flipped{g}")
-            nc.scalar.activation(flipped[:], bank[:, : m * P], COPY)
+            nc.scalar.copy(flipped[:], bank[:, : m * P])
             x_flipped.append(flipped)
 
         laps = [acc.tile([P, BANK], F32, name=f"lap{h}") for h in range(HALVES)]
-        for g, m in enumerate(GROUPS):
+        steps = [[0], [1], [2], [3, 4]]
+        for step in steps:
             for h in range(HALVES):
-                for i in range(m):
-                    nc.tensor.matmul(
-                        laps[h][:, :H],
-                        x_flipped[g][:, i * P : (i + 1) * P],
-                        lt_groups[g][:, i, h * H : (h + 1) * H],
-                        start=(g == 0 and i == 0),
-                        stop=(g == len(GROUPS) - 1 and i == m - 1),
-                    )
+                for g in step:
+                    for i in range(GROUPS[g]):
+                        nc.tensor.matmul(
+                            laps[h][:, :H],
+                            x_flipped[g][:, i * P : (i + 1) * P],
+                            lt_groups[g][:, i, h * H : (h + 1) * H],
+                            start=(g == 0 and i == 0),
+                            stop=(g == len(GROUPS) - 1 and i == GROUPS[g] - 1),
+                        )
 
         negated = held.tile([P, N], F32, name="negated")
         for h in range(HALVES):

@@ -13,10 +13,11 @@ N = 256
 HALVES = 2
 H = N // HALVES
 BANK = 512
-X_LOADS = (512, 512, 512, 512)
-assert sum(X_LOADS) == S
-GROUPS = (4, 4, 4, 2, 2)
+GROUPS = (2, 2, 4, 4, 4)
 assert sum(GROUPS) * P == S
+X_LOADS = ((0,), (1, 2), (3,), (4,))
+LAP_ORDER = (2, 3, 4, 0, 1)
+ROUND_BEHIND = (0,)
 
 FLOPS = 2 * P * S * N
 
@@ -25,44 +26,54 @@ def tile_net_kernel(tc, x, lt, tau, offs, out):
     nc = tc.nc
     with (
         tc.tile_pool(name="held", bufs=1) as held,
-        tc.psum_pool(name="flip", bufs=4) as flip,
+        tc.psum_pool(name="flip", bufs=1) as flip,
         tc.psum_pool(name="acc", bufs=1) as acc,
     ):
         x_sb = held.tile([P, S], F32, name="x_sb")
-        for q, width in enumerate(X_LOADS):
-            cols = slice(sum(X_LOADS[:q]), sum(X_LOADS[:q]) + width)
+        firsts = [sum(GROUPS[:g]) * P for g in range(len(GROUPS))]
+        for groups in X_LOADS:
+            width = sum(GROUPS[g] for g in groups) * P
+            cols = slice(firsts[groups[0]], firsts[groups[0]] + width)
             nc.sync.dma_start(x_sb[:, cols], x[:, cols])
 
-        firsts = [sum(GROUPS[:g]) * P for g in range(len(GROUPS))]
-        lt_groups = []
-        for g, (first, m) in enumerate(zip(firsts, GROUPS)):
+        lt_groups = {}
+        for g in LAP_ORDER:
+            first, m = firsts[g], GROUPS[g]
             lt_group = held.tile([P, m, N], BF16, name=f"lt_group{g}")
             rows = lt[first : first + m * P, :].rearrange("(p i) n -> p i n", i=m)
             nc.sync.dma_start(lt_group[:], rows)
-            lt_groups.append(lt_group)
+            lt_groups[g] = lt_group
 
         tau_sb = held.tile([P, 1], F32, name="tau_sb")
         nc.sync.dma_start(tau_sb[:], tau.partition_broadcast(P))
         offsets = held.tile([P, N // 16], U16, name="offsets")
         nc.sync.dma_start(offsets[:], offs)
 
-        identity = held.tile([P, P], BF16, name="identity")
-        make_identity(nc, identity[:])
+        identities = {}
+        for dtype in (F32, BF16):
+            identity = held.tile([P, P], dtype, name=f"identity{len(identities)}")
+            make_identity(nc, identity[:])
+            identities[dtype] = identity
 
         x_flipped = []
         for g, (first, m) in enumerate(zip(firsts, GROUPS)):
-            rounded = held.tile([P, m * P], BF16, name=f"rounded{g}")
-            nc.vector.tensor_copy(rounded[:], x_sb[:, first : first + m * P])
-            blocks = rounded[:].rearrange("c (k i) -> c i k", i=m)
-            bank = flip.tile([P, 2 * BANK], BF16, name="bank")
+            source = x_sb[:, first : first + m * P]
+            dtype = F32
+            if g not in ROUND_BEHIND:
+                dtype = BF16
+                rounded = held.tile([P, m * P], BF16, name=f"rounded{g}")
+                nc.vector.tensor_copy(rounded[:], source)
+                source = rounded[:]
+            blocks = source.rearrange("c (k i) -> c i k", i=m)
+            bank = flip.tile([P, BANK if dtype == F32 else 2 * BANK], dtype, name=f"bank{g}")
             for i in range(m):
-                nc.tensor.matmul(bank[:, i * P : (i + 1) * P], blocks[:, i, :], identity[:], start=True, stop=True)
+                nc.tensor.matmul(bank[:, i * P : (i + 1) * P], blocks[:, i, :], identities[dtype][:], start=True, stop=True)
             flipped = held.tile([P, m * P], BF16, name=f"flipped{g}")
             nc.scalar.copy(flipped[:], bank[:, : m * P])
             x_flipped.append(flipped)
 
         laps = [acc.tile([P, BANK], F32, name=f"lap{h}") for h in range(HALVES)]
-        steps = [[0], [1], [2], [3, 4]]
+        steps = [LAP_ORDER[:1], LAP_ORDER[1:2], LAP_ORDER[2:3], LAP_ORDER[3:]]
         for step in steps:
             for h in range(HALVES):
                 for g in step:
@@ -71,8 +82,8 @@ def tile_net_kernel(tc, x, lt, tau, offs, out):
                             laps[h][:, :H],
                             x_flipped[g][:, i * P : (i + 1) * P],
                             lt_groups[g][:, i, h * H : (h + 1) * H],
-                            start=(g == 0 and i == 0),
-                            stop=(g == len(GROUPS) - 1 and i == GROUPS[g] - 1),
+                            start=(g == LAP_ORDER[0] and i == 0),
+                            stop=(g == LAP_ORDER[-1] and i == GROUPS[g] - 1),
                         )
 
         negated = held.tile([P, N], F32, name="negated")

@@ -4,6 +4,7 @@ from concourse.masks import make_identity
 F32 = mybir.dt.float32
 BF16 = mybir.dt.bfloat16
 U16 = mybir.dt.uint16
+COPY = mybir.ActivationFunctionType.Copy
 MULT = mybir.AluOpType.mult
 ADD = mybir.AluOpType.add
 
@@ -13,10 +14,11 @@ N = 256
 HALVES = 2
 H = N // HALVES
 BANK = 512
-GROUPS = (2, 2, 4, 4, 4)
+GROUPS = (2, 2, 4, 4, 2, 2)
 assert sum(GROUPS) * P == S
-X_LOADS = ((0,), (1, 2), (3,), (4,))
-LAP_ORDER = (2, 3, 4, 0, 1)
+X_LOADS = ((0,), (1, 2), (3,), (4, 5))
+LT_LOADS = ((0, 1), (2,), (3,), (4,), (5,))
+LAP_STEPS = ((0, 1), (2,), (3,), (4, 5))
 ROUND_BEHIND = (0,)
 
 FLOPS = 2 * P * S * N
@@ -36,13 +38,13 @@ def tile_net_kernel(tc, x, lt, tau, offs, out):
             cols = slice(firsts[groups[0]], firsts[groups[0]] + width)
             nc.sync.dma_start(x_sb[:, cols], x[:, cols])
 
-        lt_groups = {}
-        for g in LAP_ORDER:
-            first, m = firsts[g], GROUPS[g]
-            lt_group = held.tile([P, m, N], BF16, name=f"lt_group{g}")
-            rows = lt[first : first + m * P, :].rearrange("(p i) n -> p i n", i=m)
-            nc.sync.dma_start(lt_group[:], rows)
-            lt_groups[g] = lt_group
+        lt_groups = []
+        for groups in LT_LOADS:
+            first, m, count = firsts[groups[0]], GROUPS[groups[0]], len(groups)
+            lt_tile = held.tile([P, count, m, N], BF16, name=f"lt_from{first}")
+            rows = lt[first : first + count * m * P, :].rearrange("(g p i) n -> p g i n", g=count, i=m)
+            nc.sync.dma_start(lt_tile[:], rows)
+            lt_groups += [lt_tile[:, k] for k in range(count)]
 
         tau_sb = held.tile([P, 1], F32, name="tau_sb")
         nc.sync.dma_start(tau_sb[:], tau.partition_broadcast(P))
@@ -73,8 +75,7 @@ def tile_net_kernel(tc, x, lt, tau, offs, out):
             x_flipped.append(flipped)
 
         laps = [acc.tile([P, BANK], F32, name=f"lap{h}") for h in range(HALVES)]
-        steps = [LAP_ORDER[:1], LAP_ORDER[1:2], LAP_ORDER[2:3], LAP_ORDER[3:]]
-        for step in steps:
+        for step in LAP_STEPS:
             for h in range(HALVES):
                 for g in step:
                     for i in range(GROUPS[g]):
@@ -82,17 +83,19 @@ def tile_net_kernel(tc, x, lt, tau, offs, out):
                             laps[h][:, :H],
                             x_flipped[g][:, i * P : (i + 1) * P],
                             lt_groups[g][:, i, h * H : (h + 1) * H],
-                            start=(g == LAP_ORDER[0] and i == 0),
-                            stop=(g == LAP_ORDER[-1] and i == GROUPS[g] - 1),
+                            start=(g == 0 and i == 0),
+                            stop=(g == len(GROUPS) - 1 and i == GROUPS[g] - 1),
                         )
 
-        negated = held.tile([P, N], F32, name="negated")
-        for h in range(HALVES):
-            nc.vector.tensor_scalar(negated[:, h * H : (h + 1) * H], laps[h][:, :H], tau_sb[:, 0:1], -1.0, MULT, MULT)
+        minus_tau = held.tile([P, 1], F32, name="minus_tau")
+        nc.vector.tensor_scalar(minus_tau[:], tau_sb[:], -1.0, None, MULT)
+        negated = [held.tile([P, H], F32, name=f"negated{h}") for h in range(HALVES)]
+        nc.vector.tensor_scalar(negated[0][:], laps[0][:, :H], minus_tau[:, 0:1], None, MULT)
+        nc.scalar.activation(negated[1][:], laps[1][:, :H], COPY, scale=minus_tau[:, 0:1])
 
         result = held.tile([P, N], F32, name="result")
         for h in range(HALVES):
             cols = slice(h * H, (h + 1) * H)
             picked = x_sb[:].indirect(offsets[:, h * H // 16 : (h + 1) * H // 16])
-            nc.vector.tensor_tensor(result[:, cols], picked, negated[:, cols], ADD)
+            nc.vector.tensor_tensor(result[:, cols], picked, negated[h][:], ADD)
             nc.sync.dma_start(out[:, cols], result[:, cols])

@@ -14,11 +14,10 @@ N = 256
 HALVES = 2
 H = N // HALVES
 BANK = 512
-GROUPS = (2, 2, 4, 4, 2, 2)
+GROUPS = (2, 4, 4, 4, 2)
 assert sum(GROUPS) * P == S
-X_LOADS = ((0,), (1, 2), (3,), (4, 5))
-LT_LOADS = ((0, 1), (2,), (3,), (4,), (5,))
-LAP_STEPS = ((0, 1), (2,), (3,), (4, 5))
+LT_ORDER = (1, 2, 3, 0, 4)
+LAP_STEPS = ((1,), (2,), (3,), (0, 4))
 ROUND_BEHIND = (0,)
 
 FLOPS = 2 * P * S * N
@@ -33,18 +32,17 @@ def tile_net_kernel(tc, x, lt, tau, offs, out):
     ):
         x_sb = held.tile([P, S], F32, name="x_sb")
         firsts = [sum(GROUPS[:g]) * P for g in range(len(GROUPS))]
-        for groups in X_LOADS:
-            width = sum(GROUPS[g] for g in groups) * P
-            cols = slice(firsts[groups[0]], firsts[groups[0]] + width)
+        for first, m in zip(firsts, GROUPS):
+            cols = slice(first, first + m * P)
             nc.sync.dma_start(x_sb[:, cols], x[:, cols])
 
-        lt_groups = []
-        for groups in LT_LOADS:
-            first, m, count = firsts[groups[0]], GROUPS[groups[0]], len(groups)
-            lt_tile = held.tile([P, count, m, N], BF16, name=f"lt_from{first}")
-            rows = lt[first : first + count * m * P, :].rearrange("(g p i) n -> p g i n", g=count, i=m)
-            nc.sync.dma_start(lt_tile[:], rows)
-            lt_groups += [lt_tile[:, k] for k in range(count)]
+        lt_groups = {}
+        for g in LT_ORDER:
+            first, m = firsts[g], GROUPS[g]
+            lt_group = held.tile([P, m, N], BF16, name=f"lt_group{g}")
+            rows = lt[first : first + m * P, :].rearrange("(p i) n -> p i n", i=m)
+            nc.sync.dma_start(lt_group[:], rows)
+            lt_groups[g] = lt_group
 
         tau_sb = held.tile([P, 1], F32, name="tau_sb")
         nc.sync.dma_start(tau_sb[:], tau.partition_broadcast(P))
@@ -83,14 +81,14 @@ def tile_net_kernel(tc, x, lt, tau, offs, out):
                             laps[h][:, :H],
                             x_flipped[g][:, i * P : (i + 1) * P],
                             lt_groups[g][:, i, h * H : (h + 1) * H],
-                            start=(g == 0 and i == 0),
-                            stop=(g == len(GROUPS) - 1 and i == GROUPS[g] - 1),
+                            start=(g == LT_ORDER[0] and i == 0),
+                            stop=(g == LT_ORDER[-1] and i == GROUPS[g] - 1),
                         )
 
         minus_tau = held.tile([P, 1], F32, name="minus_tau")
         nc.vector.tensor_scalar(minus_tau[:], tau_sb[:], -1.0, None, MULT)
         negated = [held.tile([P, H], F32, name=f"negated{h}") for h in range(HALVES)]
-        nc.vector.tensor_scalar(negated[0][:], laps[0][:, :H], minus_tau[:, 0:1], None, MULT)
+        nc.vector.tensor_scalar(negated[0][:], laps[0][:, :H], tau_sb[:, 0:1], -1.0, MULT, MULT)
         nc.scalar.activation(negated[1][:], laps[1][:, :H], COPY, scale=minus_tau[:, 0:1])
 
         result = held.tile([P, N], F32, name="result")

import concourse.mybir as mybir
from concourse.masks import make_identity

F32 = mybir.dt.float32
BF16 = mybir.dt.bfloat16
U16 = mybir.dt.uint16
COPY = mybir.ActivationFunctionType.Copy
MULT = mybir.AluOpType.mult
ADD = mybir.AluOpType.add

P = 128
S = 2048
N = 256
HALVES = 2
H = N // HALVES
BANK = 512
GROUPS = (2, 4, 4, 4, 2)
assert sum(GROUPS) * P == S
LT_ORDER = (1, 2, 3, 0, 4)
LAP_STEPS = ((1,), (2,), (3,), (0, 4))
ROUND_BEHIND = (0,)

FLOPS = 2 * P * S * N


def tile_net_kernel(tc, x, lt, tau, offs, out):
    nc = tc.nc
    with (
        tc.tile_pool(name="held", bufs=1) as held,
        tc.psum_pool(name="flip", bufs=1) as flip,
        tc.psum_pool(name="acc", bufs=1) as acc,
    ):
        x_sb = held.tile([P, S], F32, name="x_sb")
        firsts = [sum(GROUPS[:g]) * P for g in range(len(GROUPS))]
        for first, m in zip(firsts, GROUPS):
            cols = slice(first, first + m * P)
            nc.sync.dma_start(x_sb[:, cols], x[:, cols])

        lt_groups = {}
        for g in LT_ORDER:
            first, m = firsts[g], GROUPS[g]
            lt_group = held.tile([P, m, N], BF16, name=f"lt_group{g}")
            rows = lt[first : first + m * P, :].rearrange("(p i) n -> p i n", i=m)
            nc.sync.dma_start(lt_group[:], rows)
            lt_groups[g] = lt_group

        tau_sb = held.tile([P, 1], F32, name="tau_sb")
        nc.sync.dma_start(tau_sb[:], tau.partition_broadcast(P))
        offsets = held.tile([P, N // 16], U16, name="offsets")
        nc.sync.dma_start(offsets[:], offs)

        identities = {}
        for dtype in (F32, BF16):
            identity = held.tile([P, P], dtype, name=f"identity{len(identities)}")
            make_identity(nc, identity[:])
            identities[dtype] = identity

        x_flipped = []
        for g, (first, m) in enumerate(zip(firsts, GROUPS)):
            source = x_sb[:, first : first + m * P]
            dtype = F32
            if g not in ROUND_BEHIND:
                dtype = BF16
                rounded = held.tile([P, m * P], BF16, name=f"rounded{g}")
                nc.vector.tensor_copy(rounded[:], source)
                source = rounded[:]
            blocks = source.rearrange("c (k i) -> c i k", i=m)
            bank = flip.tile([P, BANK if dtype == F32 else 2 * BANK], dtype, name=f"bank{g}")
            for i in range(m):
                nc.tensor.matmul(bank[:, i * P : (i + 1) * P], blocks[:, i, :], identities[dtype][:], start=True, stop=True)
            flipped = held.tile([P, m * P], BF16, name=f"flipped{g}")
            nc.scalar.copy(flipped[:], bank[:, : m * P])
            x_flipped.append(flipped)

        laps = [acc.tile([P, BANK], F32, name=f"lap{h}") for h in range(HALVES)]
        for step in LAP_STEPS:
            for h in range(HALVES):
                for g in step:
                    for i in range(GROUPS[g]):
                        nc.tensor.matmul(
                            laps[h][:, :H],
                            x_flipped[g][:, i * P : (i + 1) * P],
                            lt_groups[g][:, i, h * H : (h + 1) * H],
                            start=(g == LT_ORDER[0] and i == 0),
                            stop=(g == LT_ORDER[-1] and i == GROUPS[g] - 1),
                        )

        minus_tau = held.tile([P, 1], F32, name="minus_tau")
        nc.vector.tensor_scalar(minus_tau[:], tau_sb[:], -1.0, None, MULT)
        negated = [held.tile([P, H], F32, name=f"negated{h}") for h in range(HALVES)]
        nc.vector.tensor_scalar(negated[0][:], laps[0][:, :H], tau_sb[:, 0:1], -1.0, MULT, MULT)
        nc.scalar.activation(negated[1][:], laps[1][:, :H], COPY, scale=minus_tau[:, 0:1])

        result = held.tile([P, N], F32, name="result")
        for h in range(HALVES):
            cols = slice(h * H, (h + 1) * H)
            picked = x_sb[:].indirect(offsets[:, h * H // 16 : (h + 1) * H // 16])
            nc.vector.tensor_tensor(result[:, cols], picked, negated[h][:], ADD)
            nc.sync.dma_start(out[:, cols], result[:, cols])
